import numpy as np
import ml_dtypes


def mxq(x, axis, fmt="e4m3"):
    dtype, down = {"e4m3": (ml_dtypes.float8_e4m3fn, 7), "e5m2": (ml_dtypes.float8_e5m2, 14)}[fmt]
    v = np.moveaxis(np.asarray(x, np.float32).astype(ml_dtypes.bfloat16).astype(np.float64), axis, -1)
    blocks = v.reshape(v.shape[:-1] + (-1, 32))
    amax = np.abs(blocks).max(-1, keepdims=True)
    byte = np.maximum(np.where(amax > 0, np.frexp(amax)[1] - 1 + 127, 0) - down, 1)
    scale = np.exp2(byte - 127.0)
    codes = (blocks / scale).astype(np.float32).astype(dtype).astype(np.float64)
    return np.moveaxis((codes * scale).reshape(v.shape), -1, axis)


WIDE = False


def mx_kscale(k):
    if not WIDE:
        return np.ones(k)
    levels = np.array([18, -18])
    if k % 512:
        return np.exp2(np.random.permutation(np.resize(levels, k // 32))).repeat(32)
    a = np.empty((k // 512, 16))
    for p in range(k // 512):
        a[p, :8] = np.random.permutation(np.resize(levels, 8))
        for g in range(8):
            far = levels[np.abs(levels - a[p, g]) >= 10]
            a[p, g + 8] = far[np.random.randint(len(far))]
    return np.exp2(a.ravel()).repeat(32)


BF16 = ml_dtypes.bfloat16


def bf(x):
    return np.asarray(x, np.float32).astype(BF16)


def f64(x):
    return np.asarray(x).astype(np.float64)


C_COUNT, ROW, COL = 8, 512, 512


def setup_inputs():
    s = mx_kscale(ROW)
    u = mx_kscale(ROW)
    return {"Pb": bf(np.random.standard_normal((C_COUNT, ROW, ROW)) * 1.25 / np.sqrt(ROW) / s),
            "Ev": bf(np.random.standard_normal((C_COUNT, ROW, ROW)) * s[:, None]),
            "W_pie": bf(np.random.standard_normal((C_COUNT, ROW, ROW)) / np.sqrt(ROW) / u),
            "feat": bf(np.random.standard_normal((C_COUNT, ROW, COL))),
            "grad_out": bf(np.random.standard_normal((C_COUNT, ROW, COL)) * 4.0
                           * np.exp2(np.random.randint(-6, 1, (C_COUNT, ROW, 1))) * u[:, None])}


def reference(Pb, Ev, W_pie, feat, grad_out):
    h = 0.3 * (f64(grad_out) * f64(feat)).sum(-1)
    dT = f64(Pb).transpose(0, 2, 1) * h[:, None, :]
    dEv = mxq(dT, 2, "e5m2") @ mxq(f64(W_pie), 2, "e4m3").transpose(0, 2, 1)
    dW = mxq(f64(Ev), 1, "e4m3").transpose(0, 2, 1) @ mxq(dT, 1, "e5m2")
    return dEv, dW

@@ -1,0 +1,165 @@
+from contextlib import ExitStack
+
+import concourse.mybir as mybir
+from concourse.masks import make_identity
+
+F32 = mybir.dt.float32
+BF16 = mybir.dt.bfloat16
+U32 = mybir.dt.uint32
+U8 = mybir.dt.uint8
+E4M3X4 = mybir.dt.float8_e4m3fn_x4
+E5M2X4 = mybir.dt.float8_e5m2_x4
+MULT = mybir.AluOpType.mult
+
+C_COUNT = 8
+D = 512
+P = 128
+R = 4
+AHEAD = 5
+
+FLOPS = C_COUNT * (2 * 2 * D * D * D + 3 * D * D)
+
+
+def tile_generator_pa_v_kernel(tc, Pb, Ev, W_pie, feat, grad_out, out_0, out_1):
+    nc = tc.nc
+    with ExitStack() as ctx:
+        const = ctx.enter_context(tc.tile_pool(name="const", bufs=1))
+        inp = ctx.enter_context(tc.tile_pool(name="inp", bufs=AHEAD))
+        mid = ctx.enter_context(tc.tile_pool(name="mid", bufs=2))
+        outp = ctx.enter_context(tc.tile_pool(name="outp", bufs=3))
+        psum_x = ctx.enter_context(tc.psum_pool(name="psum_x", bufs=2))
+        psum_o = ctx.enter_context(tc.psum_pool(name="psum_o", bufs=4))
+
+        ident = const.tile([P, P], F32, name="ident")
+        make_identity(nc, ident[:])
+
+        ctx.enter_context(tc.manual_schedule())
+
+        tiles = {}
+
+        def load(key, src, c):
+            t = inp.tile([P, R, D], BF16, name=key, tag=key)
+            nc.sync.dma_start(out=t[:], in_=src[c].rearrange("(p r) l -> p r l", r=R))
+            tiles[key, c] = t
+
+        def row_dots(c):
+            g = tiles["g", c]
+            f = tiles["f", c]
+            parts = mid.tile([P, 2, R], F32, name="parts", tag="parts")
+            for r in range(R):
+                for s in range(2):
+                    cols = slice(s * D // 2, (s + 1) * D // 2)
+                    prod = mid.tile([P, D // 2], F32, name="prod", tag="prod", bufs=4)
+                    nc.vector.scalar_tensor_tensor(
+                        out=prod[:], in0=g[:, r, cols], scalar=1.0, in1=f[:, r, cols],
+                        op0=MULT, op1=MULT, accum_out=parts[:, s, r : r + 1],
+                    )
+            tiles["parts", c] = parts
+
+        def add_parts(c):
+            parts = tiles["parts", c]
+            total = mid.tile([P, R], F32, name="total", tag="total")
+            nc.vector.tensor_add(total[:], parts[:, 0, :], parts[:, 1, :])
+            tiles["total", c] = total
+
+        def scale_total(c):
+            h = mid.tile([P, R], F32, name="h", tag="h")
+            nc.vector.tensor_scalar_mul(h[:], tiles["total", c][:], 0.3)
+            tiles["h", c] = h
+
+        def scale_rows(c):
+            pb = tiles["pb", c]
+            h = tiles["h", c]
+            dt = mid.tile([P, R, D], BF16, name="dt", tag="dt")
+            for r in range(R):
+                nc.vector.tensor_scalar(
+                    out=dt[:, r, :], in0=pb[:, r, :], scalar1=h[:, r : r + 1], scalar2=None, op0=MULT,
+                )
+            tiles["dt", c] = dt
+
+        def interleave(dst, src, c):
+            t = mid.tile([P, R, P, R], BF16, name=dst, tag=dst, align_bytes=64)
+            nc.vector.tensor_copy(out=t[:], in_=tiles[src, c][:].rearrange("p r (q m) -> p m q r", m=R))
+            tiles[dst, c] = t[:].rearrange("p m q r -> p (m q r)")
+
+        def transpose_rows(dst, src, c):
+            words = tiles[src, c][:].rearrange("p r l -> p (r l)").bitcast(F32)
+            t = mid.tile([P, D * R], BF16, name=dst, tag=dst, align_bytes=64)
+            t_words = t[:].bitcast(F32).rearrange("p (m r u) -> p m r u", r=R, u=2)
+            banks = []
+            for half in range(2):
+                bank = psum_x.tile([P, 2, 2, P], F32, name="x_" + dst, tag="x_" + dst)
+                for b in range(2):
+                    r = 2 * half + b
+                    for u in range(2):
+                        nc.tensor.transpose(bank[:, u, b, :], words[:, 256 * r + u : 256 * (r + 1) : 2], ident[:])
+                banks.append(bank)
+            for half in range(2):
+                nc.scalar.copy(
+                    out=t_words[:, :, 2 * half : 2 * half + 2, :],
+                    in_=banks[half][:].rearrange("p u b m -> p m b u"),
+                )
+            tiles[dst, c] = t[:]
+
+        def quantize(dst, src, c, fmt):
+            codes = mid.tile([P, D], U32, name=dst, tag=dst, align_bytes=64)
+            scales = mid.tile([P, D], U8, name=dst + "_s", tag=dst + "_s", align_bytes=64)
+            nc.vector.quantize_mx(out=codes[:].bitcast(fmt), scales=scales[:], in_=tiles[src, c])
+            tiles[dst, c] = (codes, scales, fmt)
+
+        def multiply(dst, lhs, rhs, c, out_ap, split):
+            lc, ls, lf = tiles[lhs, c]
+            rc, rs, rf = tiles[rhs, c]
+            o = outp.tile([P, R, D], F32, name=dst, tag=dst)
+            for m in range(R):
+                cols = slice(P * m, P * (m + 1))
+                acc = psum_o.tile([P, D], F32, name="acc", tag="acc")
+                nc.tensor.matmul_mx(
+                    out=acc[:], lhsT=lc[:, cols].bitcast(lf), lhsT_scale=ls[:, cols],
+                    rhs=rc[:].bitcast(rf), rhs_scale=rs[:], start=True, stop=True,
+                )
+                if split and m % 2:
+                    nc.vector.tensor_copy(out=o[:, m, :], in_=acc[:])
+                else:
+                    nc.scalar.copy(out=o[:, m, :], in_=acc[:])
+            nc.sync.dma_start(out=out_ap[c].rearrange("(q m) n -> q m n", m=R), in_=o[:])
+
+        srcs = {"pb": Pb, "ev": Ev, "w": W_pie, "f": feat, "g": grad_out}
+
+        for c in range(AHEAD):
+            for key in ("ev", "g", "f", "pb", "w") if c == 0 else ("w", "g", "f", "ev", "pb"):
+                load(key, srcs[key], c)
+
+        transpose_rows("wt", "w", 0)
+        for c in range(C_COUNT):
+            last = c == C_COUNT - 1
+            if c == 0:
+                interleave("evq", "ev", c)
+                row_dots(c)
+                add_parts(c)
+                quantize("ev8", "evq", c, E4M3X4)
+                scale_total(c)
+            else:
+                row_dots(c)
+                add_parts(c)
+                quantize("dtt8", "dtt", c - 1, E5M2X4)
+                multiply("o1", "ev8", "dtt8", c - 1, out_1, False)
+                scale_total(c)
+                interleave("evq", "ev", c)
+            scale_rows(c)
+            if c + AHEAD < C_COUNT:
+                for key in ("g", "f", "ev", "pb"):
+                    load(key, srcs[key], c + AHEAD)
+            transpose_rows("dtt", "dt", c)
+            if not last:
+                transpose_rows("wt", "w", c + 1)
+            if c > 0:
+                quantize("ev8", "evq", c, E4M3X4)
+            interleave("dtq", "dt", c)
+            quantize("w8", "wt", c, E4M3X4)
+            if c + AHEAD < C_COUNT:
+                load("w", W_pie, c + AHEAD)
+            quantize("dt8", "dtq", c, E5M2X4)
+            multiply("o0", "dt8", "w8", c, out_0, last)
+        quantize("dtt8", "dtt", C_COUNT - 1, E5M2X4)
+        multiply("o1", "ev8", "dtt8", C_COUNT - 1, out_1, True)

@@ -16,6 +16,7 @@ D = 512
 P = 128
 R = 4
 AHEAD = 5
+Q_VECTOR = 80
 
 FLOPS = C_COUNT * (2 * 2 * D * D * D + 3 * D * D)
 
@@ -77,10 +78,20 @@ def tile_generator_pa_v_kernel(tc, Pb, Ev, W_pie, feat, grad_out, out_0, out_1):
                 )
             tiles["dt", c] = dt
 
-        def interleave(dst, src, c):
-            t = mid.tile([P, R, P, R], BF16, name=dst, tag=dst, align_bytes=64)
-            nc.vector.tensor_copy(out=t[:], in_=tiles[src, c][:].rearrange("p r (q m) -> p m q r", m=R))
-            tiles[dst, c] = t[:].rearrange("p m q r -> p (m q r)")
+        def interleave_views(dst, src, c):
+            if (dst, c) not in tiles:
+                tiles[dst, c] = mid.tile([P, R, P, R], BF16, name=dst, tag=dst, align_bytes=64)
+            out_view = tiles[dst, c][:].rearrange("p m q r -> p q r m")
+            in_view = tiles[src, c][:].rearrange("p r (q m) -> p q r m", m=R)
+            return out_view, in_view
+
+        def interleave_v(dst, src, c, q_vector):
+            out_view, in_view = interleave_views(dst, src, c)
+            nc.vector.tensor_copy(out=out_view[:, :q_vector], in_=in_view[:, :q_vector])
+
+        def interleave_s(dst, src, c, q_vector):
+            out_view, in_view = interleave_views(dst, src, c)
+            nc.scalar.copy(out=out_view[:, q_vector:], in_=in_view[:, q_vector:])
 
         def transpose_rows(dst, src, c):
             words = tiles[src, c][:].rearrange("p r l -> p (r l)").bitcast(F32)
@@ -99,15 +110,18 @@ def tile_generator_pa_v_kernel(tc, Pb, Ev, W_pie, feat, grad_out, out_0, out_1):
                     out=t_words[:, :, 2 * half : 2 * half + 2, :],
                     in_=banks[half][:].rearrange("p u b m -> p m b u"),
                 )
-            tiles[dst, c] = t[:]
+            tiles[dst, c] = t
+
+        def flat(t):
+            return t[:].rearrange("p m q r -> p (m q r)") if len(t.shape) == 4 else t[:]
 
         def quantize(dst, src, c, fmt):
             codes = mid.tile([P, D], U32, name=dst, tag=dst, align_bytes=64)
             scales = mid.tile([P, D], U8, name=dst + "_s", tag=dst + "_s", align_bytes=64)
-            nc.vector.quantize_mx(out=codes[:].bitcast(fmt), scales=scales[:], in_=tiles[src, c])
+            nc.vector.quantize_mx(out=codes[:].bitcast(fmt), scales=scales[:], in_=flat(tiles[src, c]))
             tiles[dst, c] = (codes, scales, fmt)
 
-        def multiply(dst, lhs, rhs, c, out_ap, split):
+        def multiply(dst, lhs, rhs, c, out_ap, split, pieces):
             lc, ls, lf = tiles[lhs, c]
             rc, rs, rf = tiles[rhs, c]
             o = outp.tile([P, R, D], F32, name=dst, tag=dst)
@@ -122,44 +136,60 @@ def tile_generator_pa_v_kernel(tc, Pb, Ev, W_pie, feat, grad_out, out_0, out_1):
                     nc.vector.tensor_copy(out=o[:, m, :], in_=acc[:])
                 else:
                     nc.scalar.copy(out=o[:, m, :], in_=acc[:])
-            nc.sync.dma_start(out=out_ap[c].rearrange("(q m) n -> q m n", m=R), in_=o[:])
+            view = out_ap[c].rearrange("(q m) n -> q m n", m=R)
+            step = R // pieces
+            for m in range(0, R, step):
+                nc.sync.dma_start(out=view[:, m : m + step, :], in_=o[:, m : m + step, :])
 
         srcs = {"pb": Pb, "ev": Ev, "w": W_pie, "f": feat, "g": grad_out}
 
+        def refill(key, c):
+            if c + AHEAD < C_COUNT:
+                load(key, srcs[key], c + AHEAD)
+
         for c in range(AHEAD):
-            for key in ("ev", "g", "f", "pb", "w") if c == 0 else ("w", "g", "f", "ev", "pb"):
+            for key in ("ev", "g", "f", "w", "pb") if c == 0 else ("w", "g", "f", "ev", "pb"):
                 load(key, srcs[key], c)
 
+        interleave_v("evq", "ev", 0, Q_VECTOR)
+        interleave_s("evq", "ev", 0, Q_VECTOR)
+        refill("ev", 0)
         transpose_rows("wt", "w", 0)
+        refill("w", 0)
+        row_dots(0)
+        refill("g", 0)
+        refill("f", 0)
+        add_parts(0)
+        quantize("ev8", "evq", 0, E4M3X4)
+        scale_total(0)
+        quantize("w8", "wt", 0, E4M3X4)
         for c in range(C_COUNT):
-            last = c == C_COUNT - 1
-            if c == 0:
-                interleave("evq", "ev", c)
-                row_dots(c)
-                add_parts(c)
-                quantize("ev8", "evq", c, E4M3X4)
-                scale_total(c)
-            else:
-                row_dots(c)
-                add_parts(c)
-                quantize("dtt8", "dtt", c - 1, E5M2X4)
-                multiply("o1", "ev8", "dtt8", c - 1, out_1, False)
-                scale_total(c)
-                interleave("evq", "ev", c)
+            more = c + 1 < C_COUNT
             scale_rows(c)
-            if c + AHEAD < C_COUNT:
-                for key in ("g", "f", "ev", "pb"):
-                    load(key, srcs[key], c + AHEAD)
+            refill("pb", c)
             transpose_rows("dtt", "dt", c)
-            if not last:
+            if more:
                 transpose_rows("wt", "w", c + 1)
+                refill("w", c + 1)
             if c > 0:
                 quantize("ev8", "evq", c, E4M3X4)
-            interleave("dtq", "dt", c)
-            quantize("w8", "wt", c, E4M3X4)
-            if c + AHEAD < C_COUNT:
-                load("w", W_pie, c + AHEAD)
+            interleave_v("dtq", "dt", c, P)
+            if more:
+                interleave_s("evq", "ev", c + 1, Q_VECTOR)
+                row_dots(c + 1)
+                refill("g", c + 1)
+                refill("f", c + 1)
             quantize("dt8", "dtq", c, E5M2X4)
-            multiply("o0", "dt8", "w8", c, out_0, last)
-        quantize("dtt8", "dtt", C_COUNT - 1, E5M2X4)
-        multiply("o1", "ev8", "dtt8", C_COUNT - 1, out_1, True)
+            if more:
+                multiply("o0", "dt8", "w8", c, out_0, False, 1)
+                add_parts(c + 1)
+                quantize("dtt8", "dtt", c, E5M2X4)
+                multiply("o1", "ev8", "dtt8", c, out_1, False, 1)
+                scale_total(c + 1)
+                interleave_v("evq", "ev", c + 1, Q_VECTOR)
+                refill("ev", c + 1)
+                quantize("w8", "wt", c + 1, E4M3X4)
+            else:
+                quantize("dtt8", "dtt", c, E5M2X4)
+                multiply("o0", "dt8", "w8", c, out_0, True, 1)
+                multiply("o1", "ev8", "dtt8", c, out_1, True, 2)

@@ -37,11 +37,15 @@ def tile_generator_pa_v_kernel(tc, Pb, Ev, W_pie, feat, grad_out, out_0, out_1):
         ctx.enter_context(tc.manual_schedule())
 
         tiles = {}
+        srcs = {"pb": Pb, "ev": Ev, "w": W_pie, "f": feat, "g": grad_out}
 
-        def load(key, src, c):
+        def load(key, c):
             t = inp.tile([P, R, D], BF16, name=key, tag=key)
-            nc.sync.dma_start(out=t[:], in_=src[c].rearrange("(p r) l -> p r l", r=R))
+            nc.sync.dma_start(out=t[:], in_=rows(key, c))
             tiles[key, c] = t
+
+        def rows(key, c):
+            return srcs[key][c].rearrange("(p r) l -> p r l", r=R)
 
         def row_dots(c):
             g = tiles["g", c]
@@ -141,33 +145,43 @@ def tile_generator_pa_v_kernel(tc, Pb, Ev, W_pie, feat, grad_out, out_0, out_1):
             for m in range(0, R, step):
                 nc.sync.dma_start(out=view[:, m : m + step, :], in_=o[:, m : m + step, :])
 
-        srcs = {"pb": Pb, "ev": Ev, "w": W_pie, "f": feat, "g": grad_out}
-
         def refill(key, c):
             if c + AHEAD < C_COUNT:
-                load(key, srcs[key], c + AHEAD)
+                load(key, c + AHEAD)
 
-        for c in range(AHEAD):
-            for key in ("ev", "g", "f", "w", "pb") if c == 0 else ("w", "g", "f", "ev", "pb"):
-                load(key, srcs[key], c)
+        tiles["g", 0] = inp.tile([P, R, D], BF16, name="g", tag="g")
+        tiles["f", 0] = inp.tile([P, R, D], BF16, name="f", tag="f")
+        for r in range(0, R, 2):
+            for key in ("g", "f"):
+                nc.sync.dma_start(out=tiles[key, 0][:, r : r + 2, :], in_=rows(key, 0)[:, r : r + 2, :])
+        load("ev", 0)
+        load("pb", 0)
+        for c in range(1, AHEAD):
+            load("g", c)
+            load("f", c)
+            if c == 1:
+                load("w", 0)
+            load("w", c)
+            load("ev", c)
+            load("pb", c)
 
-        interleave_v("evq", "ev", 0, Q_VECTOR)
-        interleave_s("evq", "ev", 0, Q_VECTOR)
-        refill("ev", 0)
-        transpose_rows("wt", "w", 0)
-        refill("w", 0)
         row_dots(0)
         refill("g", 0)
         refill("f", 0)
+        interleave_v("evq", "ev", 0, Q_VECTOR)
+        interleave_s("evq", "ev", 0, Q_VECTOR)
+        refill("ev", 0)
         add_parts(0)
         quantize("ev8", "evq", 0, E4M3X4)
         scale_total(0)
-        quantize("w8", "wt", 0, E4M3X4)
         for c in range(C_COUNT):
             more = c + 1 < C_COUNT
             scale_rows(c)
             refill("pb", c)
             transpose_rows("dtt", "dt", c)
+            if c == 0:
+                transpose_rows("wt", "w", 0)
+                refill("w", 0)
             if more:
                 transpose_rows("wt", "w", c + 1)
                 refill("w", c + 1)
@@ -180,6 +194,8 @@ def tile_generator_pa_v_kernel(tc, Pb, Ev, W_pie, feat, grad_out, out_0, out_1):
                 refill("g", c + 1)
                 refill("f", c + 1)
             quantize("dt8", "dtq", c, E5M2X4)
+            if c == 0:
+                quantize("w8", "wt", 0, E4M3X4)
             if more:
                 multiply("o0", "dt8", "w8", c, out_0, False, 1)
                 add_parts(c + 1)

from contextlib import ExitStack

import concourse.mybir as mybir
from concourse.masks import make_identity

F32 = mybir.dt.float32
BF16 = mybir.dt.bfloat16
U32 = mybir.dt.uint32
U8 = mybir.dt.uint8
E4M3X4 = mybir.dt.float8_e4m3fn_x4
E5M2X4 = mybir.dt.float8_e5m2_x4
MULT = mybir.AluOpType.mult

C_COUNT = 8
D = 512
P = 128
R = 4
AHEAD = 5
Q_VECTOR = 80

FLOPS = C_COUNT * (2 * 2 * D * D * D + 3 * D * D)


def tile_generator_pa_v_kernel(tc, Pb, Ev, W_pie, feat, grad_out, out_0, out_1):
    nc = tc.nc
    with ExitStack() as ctx:
        const = ctx.enter_context(tc.tile_pool(name="const", bufs=1))
        inp = ctx.enter_context(tc.tile_pool(name="inp", bufs=AHEAD))
        mid = ctx.enter_context(tc.tile_pool(name="mid", bufs=2))
        outp = ctx.enter_context(tc.tile_pool(name="outp", bufs=3))
        psum_x = ctx.enter_context(tc.psum_pool(name="psum_x", bufs=2))
        psum_o = ctx.enter_context(tc.psum_pool(name="psum_o", bufs=4))

        ident = const.tile([P, P], F32, name="ident")
        make_identity(nc, ident[:])

        ctx.enter_context(tc.manual_schedule())

        tiles = {}
        srcs = {"pb": Pb, "ev": Ev, "w": W_pie, "f": feat, "g": grad_out}

        def load(key, c):
            t = inp.tile([P, R, D], BF16, name=key, tag=key)
            nc.sync.dma_start(out=t[:], in_=rows(key, c))
            tiles[key, c] = t

        def rows(key, c):
            return srcs[key][c].rearrange("(p r) l -> p r l", r=R)

        def row_dots(c):
            g = tiles["g", c]
            f = tiles["f", c]
            parts = mid.tile([P, 2, R], F32, name="parts", tag="parts")
            for r in range(R):
                for s in range(2):
                    cols = slice(s * D // 2, (s + 1) * D // 2)
                    prod = mid.tile([P, D // 2], F32, name="prod", tag="prod", bufs=4)
                    nc.vector.scalar_tensor_tensor(
                        out=prod[:], in0=g[:, r, cols], scalar=1.0, in1=f[:, r, cols],
                        op0=MULT, op1=MULT, accum_out=parts[:, s, r : r + 1],
                    )
            tiles["parts", c] = parts

        def add_parts(c):
            parts = tiles["parts", c]
            total = mid.tile([P, R], F32, name="total", tag="total")
            nc.vector.tensor_add(total[:], parts[:, 0, :], parts[:, 1, :])
            tiles["total", c] = total

        def scale_total(c):
            h = mid.tile([P, R], F32, name="h", tag="h")
            nc.vector.tensor_scalar_mul(h[:], tiles["total", c][:], 0.3)
            tiles["h", c] = h

        def scale_rows(c):
            pb = tiles["pb", c]
            h = tiles["h", c]
            dt = mid.tile([P, R, D], BF16, name="dt", tag="dt")
            for r in range(R):
                nc.vector.tensor_scalar(
                    out=dt[:, r, :], in0=pb[:, r, :], scalar1=h[:, r : r + 1], scalar2=None, op0=MULT,
                )
            tiles["dt", c] = dt

        def interleave_views(dst, src, c):
            if (dst, c) not in tiles:
                tiles[dst, c] = mid.tile([P, R, P, R], BF16, name=dst, tag=dst, align_bytes=64)
            out_view = tiles[dst, c][:].rearrange("p m q r -> p q r m")
            in_view = tiles[src, c][:].rearrange("p r (q m) -> p q r m", m=R)
            return out_view, in_view

        def interleave_v(dst, src, c, q_vector):
            out_view, in_view = interleave_views(dst, src, c)
            nc.vector.tensor_copy(out=out_view[:, :q_vector], in_=in_view[:, :q_vector])

        def interleave_s(dst, src, c, q_vector):
            out_view, in_view = interleave_views(dst, src, c)
            nc.scalar.copy(out=out_view[:, q_vector:], in_=in_view[:, q_vector:])

        def transpose_rows(dst, src, c):
            words = tiles[src, c][:].rearrange("p r l -> p (r l)").bitcast(F32)
            t = mid.tile([P, D * R], BF16, name=dst, tag=dst, align_bytes=64)
            t_words = t[:].bitcast(F32).rearrange("p (m r u) -> p m r u", r=R, u=2)
            banks = []
            for half in range(2):
                bank = psum_x.tile([P, 2, 2, P], F32, name="x_" + dst, tag="x_" + dst)
                for b in range(2):
                    r = 2 * half + b
                    for u in range(2):
                        nc.tensor.transpose(bank[:, u, b, :], words[:, 256 * r + u : 256 * (r + 1) : 2], ident[:])
                banks.append(bank)
            for half in range(2):
                nc.scalar.copy(
                    out=t_words[:, :, 2 * half : 2 * half + 2, :],
                    in_=banks[half][:].rearrange("p u b m -> p m b u"),
                )
            tiles[dst, c] = t

        def flat(t):
            return t[:].rearrange("p m q r -> p (m q r)") if len(t.shape) == 4 else t[:]

        def quantize(dst, src, c, fmt):
            codes = mid.tile([P, D], U32, name=dst, tag=dst, align_bytes=64)
            scales = mid.tile([P, D], U8, name=dst + "_s", tag=dst + "_s", align_bytes=64)
            nc.vector.quantize_mx(out=codes[:].bitcast(fmt), scales=scales[:], in_=flat(tiles[src, c]))
            tiles[dst, c] = (codes, scales, fmt)

        def multiply(dst, lhs, rhs, c, out_ap, split, pieces):
            lc, ls, lf = tiles[lhs, c]
            rc, rs, rf = tiles[rhs, c]
            o = outp.tile([P, R, D], F32, name=dst, tag=dst)
            for m in range(R):
                cols = slice(P * m, P * (m + 1))
                acc = psum_o.tile([P, D], F32, name="acc", tag="acc")
                nc.tensor.matmul_mx(
                    out=acc[:], lhsT=lc[:, cols].bitcast(lf), lhsT_scale=ls[:, cols],
                    rhs=rc[:].bitcast(rf), rhs_scale=rs[:], start=True, stop=True,
                )
                if split and m % 2:
                    nc.vector.tensor_copy(out=o[:, m, :], in_=acc[:])
                else:
                    nc.scalar.copy(out=o[:, m, :], in_=acc[:])
            view = out_ap[c].rearrange("(q m) n -> q m n", m=R)
            step = R // pieces
            for m in range(0, R, step):
                nc.sync.dma_start(out=view[:, m : m + step, :], in_=o[:, m : m + step, :])

        def refill(key, c):
            if c + AHEAD < C_COUNT:
                load(key, c + AHEAD)

        tiles["g", 0] = inp.tile([P, R, D], BF16, name="g", tag="g")
        tiles["f", 0] = inp.tile([P, R, D], BF16, name="f", tag="f")
        for r in range(0, R, 2):
            for key in ("g", "f"):
                nc.sync.dma_start(out=tiles[key, 0][:, r : r + 2, :], in_=rows(key, 0)[:, r : r + 2, :])
        load("ev", 0)
        load("pb", 0)
        for c in range(1, AHEAD):
            load("g", c)
            load("f", c)
            if c == 1:
                load("w", 0)
            load("w", c)
            load("ev", c)
            load("pb", c)

        row_dots(0)
        refill("g", 0)
        refill("f", 0)
        interleave_v("evq", "ev", 0, Q_VECTOR)
        interleave_s("evq", "ev", 0, Q_VECTOR)
        refill("ev", 0)
        add_parts(0)
        quantize("ev8", "evq", 0, E4M3X4)
        scale_total(0)
        for c in range(C_COUNT):
            more = c + 1 < C_COUNT
            scale_rows(c)
            refill("pb", c)
            transpose_rows("dtt", "dt", c)
            if c == 0:
                transpose_rows("wt", "w", 0)
                refill("w", 0)
            if more:
                transpose_rows("wt", "w", c + 1)
                refill("w", c + 1)
            if c > 0:
                quantize("ev8", "evq", c, E4M3X4)
            interleave_v("dtq", "dt", c, P)
            if more:
                interleave_s("evq", "ev", c + 1, Q_VECTOR)
                row_dots(c + 1)
                refill("g", c + 1)
                refill("f", c + 1)
            quantize("dt8", "dtq", c, E5M2X4)
            if c == 0:
                quantize("w8", "wt", 0, E4M3X4)
            if more:
                multiply("o0", "dt8", "w8", c, out_0, False, 1)
                add_parts(c + 1)
                quantize("dtt8", "dtt", c, E5M2X4)
                multiply("o1", "ev8", "dtt8", c, out_1, False, 1)
                scale_total(c + 1)
                interleave_v("evq", "ev", c + 1, Q_VECTOR)
                refill("ev", c + 1)
                quantize("w8", "wt", c + 1, E4M3X4)
            else:
                quantize("dtt8", "dtt", c, E5M2X4)
                multiply("o0", "dt8", "w8", c, out_0, True, 1)
                multiply("o1", "ev8", "dtt8", c, out_1, True, 2)
